import numpy as np
import ml_dtypes


def mxq(x, axis, fmt="e4m3"):
    dtype, down = {"e4m3": (ml_dtypes.float8_e4m3fn, 7), "e5m2": (ml_dtypes.float8_e5m2, 14)}[fmt]
    v = np.moveaxis(np.asarray(x, np.float32).astype(ml_dtypes.bfloat16).astype(np.float64), axis, -1)
    blocks = v.reshape(v.shape[:-1] + (-1, 32))
    amax = np.abs(blocks).max(-1, keepdims=True)
    byte = np.maximum(np.where(amax > 0, np.frexp(amax)[1] - 1 + 127, 0) - down, 1)
    scale = np.exp2(byte - 127.0)
    codes = (blocks / scale).astype(np.float32).astype(dtype).astype(np.float64)
    return np.moveaxis((codes * scale).reshape(v.shape), -1, axis)


WIDE = False


def mx_kscale(k):
    if not WIDE:
        return np.ones(k)
    levels = np.array([10, -10, 5, -5, 0])
    a = np.random.permutation(np.resize(levels, k // 512 * 4)).reshape(k // 512, 4)
    idx = np.arange(k)
    return np.exp2(a[idx // 512, idx % 128 // 32])


BF16 = ml_dtypes.bfloat16


def bf(x):
    return np.asarray(x, np.float32).astype(BF16)


def f64(x):
    return np.asarray(x).astype(np.float64)


E2M1 = np.array([0.0, 0.5, 1.0, 1.5, 2.0, 3.0, 4.0, 6.0, -0.0, -0.5, -1.0, -1.5, -2.0, -3.0, -4.0, -6.0])


def pack_weight(w, fmt):
    k, n = w.shape
    w = f64(bf(w)).reshape(k // 32, 32, n)
    amax = np.abs(w).max(1)
    if fmt == "e4m3":
        byte = np.frexp(amax)[1] - 1 + 127 - 7
    else:
        mant, ex = np.frexp(amax / 6.0)
        byte = np.where(mant > 0.5, ex, ex - 1) + 127
    byte = np.clip(np.where(amax > 0, byte, 1), 1, 254)
    scaled = (w * np.exp2(127.0 - byte)[:, None, :]).reshape(k, n).astype(np.float32)
    by_word = np.ascontiguousarray(scaled.reshape(k // 512, 128, 4, n).transpose(0, 1, 3, 2))
    if fmt == "e4m3":
        words = by_word.astype(ml_dtypes.float8_e4m3fn).view(np.uint8)
    else:
        c = by_word.astype(ml_dtypes.float4_e2m1fn).view(np.uint8) & 0xF
        words = c[..., 0::2] | (c[..., 1::2] << 4)
    return np.ascontiguousarray(words), np.ascontiguousarray(byte.astype(np.uint8).reshape(k // 512, 16, n))


def unpack_weight(words, scales, fmt):
    g, p, n, _ = words.shape
    if fmt == "e4m3":
        vals = np.ascontiguousarray(words).view(ml_dtypes.float8_e4m3fn).astype(np.float64)
    else:
        nib = np.empty((g, p, n, 4), np.uint8)
        nib[..., 0::2] = words & 0xF
        nib[..., 1::2] = words >> 4
        vals = E2M1[nib]
    vals = vals * np.repeat(np.exp2(scales.astype(np.float64) - 127.0), 8, axis=1)[..., None]
    return vals.transpose(0, 1, 3, 2).reshape(g * 512, n)

def pack4(w):
    words, scales = pack_weight(w, "e2m1")
    return words.reshape(words.shape[0], 128, -1), scales


def unpack4(words, scales):
    return unpack_weight(words.reshape(words.shape[0], 128, -1, 2), scales, "e2m1")


B, T, D, H, HD = 2, 64, 8192, 8, 128
E = H * HD
HALF = HD // 2


def rotate_half(u):
    return np.concatenate((-u[..., HALF:], u[..., :HALF]), axis=-1)


def setup_inputs():
    s = mx_kscale(D)
    x = bf(np.random.standard_normal((B, T, D)) * s)
    rope_cos = bf(np.random.random_sample((1, 1, T, HD)))
    rope_sin = bf(np.random.random_sample((1, 1, T, HD)))
    w = np.random.standard_normal((3 * E, D)) / np.sqrt(D) / s[None, :]
    words, scales = pack4(np.ascontiguousarray(w.T))
    qkv_b = bf(np.random.standard_normal(3 * E) * 0.3)
    return {"x": x,
            "rope_cos": rope_cos,
            "rope_sin": rope_sin,
            "qkv_w_words": words,
            "qkv_w_scales": scales,
            "qkv_b": qkv_b}


def reference(x, rope_cos, rope_sin, qkv_w_words, qkv_w_scales, qkv_b):
    qkv = (mxq(f64(x), 2, "e4m3") @ unpack4(qkv_w_words, qkv_w_scales)) + f64(qkv_b)
    qkv = qkv.reshape(B, T, 3, H, HD).transpose(2, 0, 3, 1, 4)
    q, k, v = qkv[0], qkv[1], qkv[2]
    cos = f64(rope_cos)[:, :, :T, :]
    sin = f64(rope_sin)[:, :, :T, :]
    q_rot = q * cos + rotate_half(q) * sin
    k_rot = k * cos + rotate_half(k) * sin
    return q_rot, k_rot, v

@@ -1,0 +1,186 @@
+from contextlib import ExitStack
+
+import concourse.mybir as mybir
+from concourse.masks import make_identity
+
+F32 = mybir.dt.float32
+BF16 = mybir.dt.bfloat16
+I32 = mybir.dt.int32
+U32 = mybir.dt.uint32
+U8 = mybir.dt.uint8
+FP8X4 = mybir.dt.float8_e4m3fn_x4
+FP4X4 = mybir.dt.float4_e2m1fn_x4
+ADD = mybir.AluOpType.add
+MULT = mybir.AluOpType.mult
+
+P = 128
+PACK = 4
+K_PASS = P * PACK
+
+BATCH, SEQ, D_MODEL = 2, 64, 8192
+HEADS, HEAD_DIM = 8, 128
+HALF_DIM = HEAD_DIM // 2
+STREAMS = 3
+ROTATED_STREAMS = 2
+STREAM_COLS = HEADS * HEAD_DIM
+QKV_COLS = STREAMS * STREAM_COLS
+GROUPS = D_MODEL // K_PASS
+
+BANK_COLS = 512
+BANKS = 8
+BANKS_PER_STREAM = STREAM_COLS // BANK_COLS
+HEADS_PER_BANK = BANK_COLS // HEAD_DIM
+FP4_WORD_BYTES = 2
+
+WORDS_PER_GROUP = K_PASS // 2
+GROUPS_PER_BANK = 2
+GROUPS_PER_X_LOAD = 4
+GROUPS_PER_SCALE_LOAD = 4
+GROUPS_PER_WORD_LOAD = 2
+
+FLOPS = 2 * BATCH * SEQ * D_MODEL * QKV_COLS
+
+
+def tile_causalselfattention_pa_k_kernel(
+    tc, x, rope_cos, rope_sin, qkv_w_words, qkv_w_scales, qkv_b, out_0, out_1, out_2
+):
+    nc = tc.nc
+    outs = [out_0, out_1, out_2]
+
+    with ExitStack() as ctx:
+        ctx.enter_context(tc.manual_schedule())
+        keep = ctx.enter_context(tc.tile_pool(name="keep", bufs=1))
+        work = ctx.enter_context(tc.tile_pool(name="work", bufs=3))
+        psum = ctx.enter_context(tc.psum_pool(name="psum", bufs=BANKS))
+
+        x_sb = keep.tile([P, D_MODEL], BF16)
+        x_grouped = keep.tile([P, GROUPS, P, PACK], BF16, align_bytes=64)
+        x_codes = keep.tile([P, GROUPS, P], U32, align_bytes=64)
+        x_scales = keep.tile([P, GROUPS, P], U8, align_bytes=64)
+        w_words = keep.tile([P, STREAMS, GROUPS, STREAM_COLS * FP4_WORD_BYTES], U8, align_bytes=64)
+        w_scales = keep.tile([P, GROUPS, QKV_COLS], U8, align_bytes=64)
+        identity = keep.tile([P, P], F32)
+        ones = keep.tile([P, P], BF16)
+        bias_rows = keep.tile([P, QKV_COLS], BF16)
+        bias_all = keep.tile([P, QKV_COLS], BF16)
+        cos_sb = keep.tile([P, HEAD_DIM], BF16)
+        sin_sb = keep.tile([P, HEAD_DIM], BF16)
+
+        for c in range(GROUPS // GROUPS_PER_X_LOAD):
+            cols = slice(c * GROUPS_PER_X_LOAD * K_PASS, (c + 1) * GROUPS_PER_X_LOAD * K_PASS)
+            for b in range(BATCH):
+                nc.sync.dma_start(out=x_sb[b:P:BATCH, cols], in_=x[b, :, cols])
+
+        nc.vector.memset(bias_rows[:], 0.0)
+        nc.vector.memset(ones[:], 1.0)
+        nc.scalar.dma_start(out=bias_rows[0:1, :], in_=qkv_b.rearrange("(o n) -> o n", o=1))
+        for b in range(BATCH):
+            nc.scalar.dma_start(out=cos_sb[b:P:BATCH, :], in_=rope_cos[0, 0])
+            nc.scalar.dma_start(out=sin_sb[b:P:BATCH, :], in_=rope_sin[0, 0])
+        make_identity(nc, identity[:])
+
+        for s in range(GROUPS // GROUPS_PER_SCALE_LOAD):
+            groups = slice(s * GROUPS_PER_SCALE_LOAD, (s + 1) * GROUPS_PER_SCALE_LOAD)
+            nc.vector.memset(w_scales[:, groups, :].bitcast(I32), 0)
+            for i in range(8):
+                first_partition = 32 * (i // 4) + i % 4
+                nc.sync.dma_start(
+                    out=w_scales[first_partition:P:64, groups, :].bitcast(I32),
+                    in_=qkv_w_scales[groups, i:16:8, :].bitcast(I32).rearrange("g i n -> i g n"),
+                )
+
+        for j in range(STREAMS):
+            stream_bytes = slice(
+                j * STREAM_COLS * FP4_WORD_BYTES, (j + 1) * STREAM_COLS * FP4_WORD_BYTES
+            )
+            for c in range(GROUPS // GROUPS_PER_WORD_LOAD):
+                groups = slice(c * GROUPS_PER_WORD_LOAD, (c + 1) * GROUPS_PER_WORD_LOAD)
+                nc.sync.dma_start(
+                    out=w_words[:, j, groups, :].bitcast(I32),
+                    in_=qkv_w_words[groups, :, stream_bytes].bitcast(I32).rearrange("g p n -> p g n"),
+                )
+
+        x_words = x_sb[:].bitcast(F32)
+        for c in range(GROUPS // GROUPS_PER_X_LOAD):
+            for bank in range(GROUPS_PER_X_LOAD // GROUPS_PER_BANK):
+                first_group = c * GROUPS_PER_X_LOAD + bank * GROUPS_PER_BANK
+                x_t = psum.tile([P, GROUPS_PER_BANK, 2, P], F32, tag="bank")
+                for i in range(GROUPS_PER_BANK):
+                    first_word = (first_group + i) * WORDS_PER_GROUP
+                    for u in range(2):
+                        nc.tensor.transpose(
+                            x_t[:, i, u, :],
+                            x_words[:, first_word + u : first_word + WORDS_PER_GROUP : 2],
+                            identity[:],
+                        )
+                nc.scalar.copy(
+                    out=x_grouped[:, first_group : first_group + GROUPS_PER_BANK, :, :].bitcast(F32),
+                    in_=x_t[:].rearrange("p g u r -> p g r u"),
+                )
+            groups = slice(c * GROUPS_PER_X_LOAD, (c + 1) * GROUPS_PER_X_LOAD)
+            nc.vector.quantize_mx(
+                out=x_codes[:, groups, :].rearrange("p g r -> p (g r)").bitcast(FP8X4),
+                scales=x_scales[:, groups, :].rearrange("p g r -> p (g r)"),
+                in_=x_grouped[:, groups, :, :].rearrange("p g r t -> p (g r t)"),
+            )
+
+        for n in range(QKV_COLS // BANK_COLS):
+            cols = slice(n * BANK_COLS, (n + 1) * BANK_COLS)
+            bias_bank = psum.tile([P, BANK_COLS], F32, tag="bank")
+            nc.tensor.matmul(out=bias_bank[:], lhsT=ones[:], rhs=bias_rows[:, cols], start=True, stop=True)
+            nc.scalar.copy(out=bias_all[:, cols], in_=bias_bank[:])
+
+        nc.vector.tensor_scalar_mul(out=sin_sb[:, 0:HALF_DIM], in0=sin_sb[:, 0:HALF_DIM], scalar1=-1.0)
+        cos_heads = cos_sb[:].unsqueeze(1).to_broadcast([P, HEADS_PER_BANK, HEAD_DIM])
+        sin_heads = sin_sb[:].unsqueeze(1).to_broadcast([P, HEADS_PER_BANK, HEAD_DIM])
+        low = slice(0, HALF_DIM)
+        high = slice(HALF_DIM, HEAD_DIM)
+
+        for j in range(STREAMS):
+            acc = [
+                psum.tile([P, BANK_COLS], F32, tag="bank", name="acc_%d_%d" % (j, n))
+                for n in range(BANKS_PER_STREAM)
+            ]
+            for g in range(GROUPS):
+                for n in range(BANKS_PER_STREAM):
+                    word_bytes = slice(
+                        n * BANK_COLS * FP4_WORD_BYTES, (n + 1) * BANK_COLS * FP4_WORD_BYTES
+                    )
+                    qkv_col = j * STREAM_COLS + n * BANK_COLS
+                    nc.tensor.matmul_mx(
+                        out=acc[n][:],
+                        lhsT=x_codes[:, g, :].bitcast(FP8X4),
+                        lhsT_scale=x_scales[:, g, :],
+                        rhs=w_words[:, j, g, word_bytes].bitcast(FP4X4),
+                        rhs_scale=w_scales[:, g, qkv_col : qkv_col + BANK_COLS],
+                        start=(g == 0),
+                        stop=(g == GROUPS - 1),
+                    )
+
+            for n in range(BANKS_PER_STREAM):
+                qkv_col = j * STREAM_COLS + n * BANK_COLS
+                biased = work.tile([P, HEADS_PER_BANK, HEAD_DIM], F32)
+                nc.vector.tensor_tensor(
+                    out=biased[:].rearrange("p h d -> p (h d)"),
+                    in0=acc[n][:],
+                    in1=bias_all[:, qkv_col : qkv_col + BANK_COLS],
+                    op=ADD,
+                )
+                finished = biased
+                if j < ROTATED_STREAMS:
+                    turned = work.tile([P, HEADS_PER_BANK, HEAD_DIM], F32)
+                    nc.vector.tensor_tensor(
+                        out=turned[:, :, low], in0=biased[:, :, high], in1=sin_heads[:, :, low], op=MULT
+                    )
+                    nc.vector.tensor_tensor(
+                        out=turned[:, :, high], in0=biased[:, :, low], in1=sin_heads[:, :, high], op=MULT
+                    )
+                    rotated = work.tile([P, HEADS_PER_BANK, HEAD_DIM], F32)
+                    nc.vector.tensor_tensor(out=rotated[:], in0=biased[:], in1=cos_heads, op=MULT)
+                    nc.vector.tensor_tensor(out=rotated[:], in0=rotated[:], in1=turned[:], op=ADD)
+                    finished = rotated
+                heads = slice(n * HEADS_PER_BANK, (n + 1) * HEADS_PER_BANK)
+                for b in range(BATCH):
+                    nc.scalar.dma_start(
+                        out=outs[j][b, heads].rearrange("h t d -> t h d"), in_=finished[b:P:BATCH, :, :]
+                    )

@@ -181,6 +181,6 @@ def tile_causalselfattention_pa_k_kernel(
                     finished = rotated
                 heads = slice(n * HEADS_PER_BANK, (n + 1) * HEADS_PER_BANK)
                 for b in range(BATCH):
-                    nc.scalar.dma_start(
+                    nc.sync.dma_start(
                         out=outs[j][b, heads].rearrange("h t d -> t h d"), in_=finished[b:P:BATCH, :, :]
                     )

@@ -58,7 +58,10 @@ def tile_causalselfattention_pa_k_kernel(
         x_codes = keep.tile([P, GROUPS, P], U32, align_bytes=64)
         x_scales = keep.tile([P, GROUPS, P], U8, align_bytes=64)
         w_words = keep.tile([P, STREAMS, GROUPS, STREAM_COLS * FP4_WORD_BYTES], U8, align_bytes=64)
-        w_scales = keep.tile([P, GROUPS, QKV_COLS], U8, align_bytes=64)
+        w_scales = [
+            keep.tile([P, GROUPS_PER_SCALE_LOAD, QKV_COLS], U8, align_bytes=64, name="w_scales_%d" % s)
+            for s in range(GROUPS // GROUPS_PER_SCALE_LOAD)
+        ]
         identity = keep.tile([P, P], F32)
         ones = keep.tile([P, P], BF16)
         bias_rows = keep.tile([P, QKV_COLS], BF16)
@@ -71,21 +74,21 @@ def tile_causalselfattention_pa_k_kernel(
             for b in range(BATCH):
                 nc.sync.dma_start(out=x_sb[b:P:BATCH, cols], in_=x[b, :, cols])
 
-        nc.vector.memset(bias_rows[:], 0.0)
-        nc.vector.memset(ones[:], 1.0)
-        nc.scalar.dma_start(out=bias_rows[0:1, :], in_=qkv_b.rearrange("(o n) -> o n", o=1))
-        for b in range(BATCH):
-            nc.scalar.dma_start(out=cos_sb[b:P:BATCH, :], in_=rope_cos[0, 0])
-            nc.scalar.dma_start(out=sin_sb[b:P:BATCH, :], in_=rope_sin[0, 0])
         make_identity(nc, identity[:])
+        nc.vector.memset(ones[:], 1.0)
+        nc.scalar.mul(bias_rows[:], ones[:, 0:1].to_broadcast([P, QKV_COLS]), 0.0)
+        for b in range(BATCH):
+            nc.gpsimd.dma_start(out=cos_sb[b:P:BATCH, :], in_=rope_cos[0, 0])
+            nc.gpsimd.dma_start(out=sin_sb[b:P:BATCH, :], in_=rope_sin[0, 0])
+        nc.gpsimd.dma_start(out=bias_rows[0:1, :], in_=qkv_b.rearrange("(o n) -> o n", o=1))
 
         for s in range(GROUPS // GROUPS_PER_SCALE_LOAD):
             groups = slice(s * GROUPS_PER_SCALE_LOAD, (s + 1) * GROUPS_PER_SCALE_LOAD)
-            nc.vector.memset(w_scales[:, groups, :].bitcast(I32), 0)
+            nc.vector.memset(w_scales[s][:].bitcast(I32), 0)
             for i in range(8):
                 first_partition = 32 * (i // 4) + i % 4
                 nc.sync.dma_start(
-                    out=w_scales[first_partition:P:64, groups, :].bitcast(I32),
+                    out=w_scales[s][first_partition:P:64, :, :].bitcast(I32),
                     in_=qkv_w_scales[groups, i:16:8, :].bitcast(I32).rearrange("g i n -> i g n"),
                 )
 
@@ -93,8 +96,11 @@ def tile_causalselfattention_pa_k_kernel(
             stream_bytes = slice(
                 j * STREAM_COLS * FP4_WORD_BYTES, (j + 1) * STREAM_COLS * FP4_WORD_BYTES
             )
-            for c in range(GROUPS // GROUPS_PER_WORD_LOAD):
-                groups = slice(c * GROUPS_PER_WORD_LOAD, (c + 1) * GROUPS_PER_WORD_LOAD)
+            starts = list(range(0, GROUPS, GROUPS_PER_WORD_LOAD)) + [GROUPS]
+            if j == STREAMS - 1:
+                starts = starts[:-1] + [GROUPS - 1, GROUPS]
+            for first, end in zip(starts[:-1], starts[1:]):
+                groups = slice(first, end)
                 nc.sync.dma_start(
                     out=w_words[:, j, groups, :].bitcast(I32),
                     in_=qkv_w_words[groups, :, stream_bytes].bitcast(I32).rearrange("g p n -> p g n"),
@@ -152,12 +158,14 @@ def tile_causalselfattention_pa_k_kernel(
                         lhsT=x_codes[:, g, :].bitcast(FP8X4),
                         lhsT_scale=x_scales[:, g, :],
                         rhs=w_words[:, j, g, word_bytes].bitcast(FP4X4),
-                        rhs_scale=w_scales[:, g, qkv_col : qkv_col + BANK_COLS],
+                        rhs_scale=w_scales[g // GROUPS_PER_SCALE_LOAD][:, g % GROUPS_PER_SCALE_LOAD, qkv_col : qkv_col + BANK_COLS],
                         start=(g == 0),
                         stop=(g == GROUPS - 1),
                     )
 
-            for n in range(BANKS_PER_STREAM):
+            banks = range(BANKS_PER_STREAM)
+            finished = []
+            for n in banks:
                 qkv_col = j * STREAM_COLS + n * BANK_COLS
                 biased = work.tile([P, HEADS_PER_BANK, HEAD_DIM], F32)
                 nc.vector.tensor_tensor(
@@ -166,21 +174,24 @@ def tile_causalselfattention_pa_k_kernel(
                     in1=bias_all[:, qkv_col : qkv_col + BANK_COLS],
                     op=ADD,
                 )
-                finished = biased
-                if j < ROTATED_STREAMS:
-                    turned = work.tile([P, HEADS_PER_BANK, HEAD_DIM], F32)
-                    nc.vector.tensor_tensor(
-                        out=turned[:, :, low], in0=biased[:, :, high], in1=sin_heads[:, :, low], op=MULT
-                    )
-                    nc.vector.tensor_tensor(
-                        out=turned[:, :, high], in0=biased[:, :, low], in1=sin_heads[:, :, high], op=MULT
-                    )
-                    rotated = work.tile([P, HEADS_PER_BANK, HEAD_DIM], F32)
-                    nc.vector.tensor_tensor(out=rotated[:], in0=biased[:], in1=cos_heads, op=MULT)
-                    nc.vector.tensor_tensor(out=rotated[:], in0=rotated[:], in1=turned[:], op=ADD)
-                    finished = rotated
+                finished.append(biased)
+            if j < ROTATED_STREAMS:
+                turned = [work.tile([P, HEADS_PER_BANK, HEAD_DIM], F32, tag="turned", name="turned_%d" % n) for n in banks]
+                rotated = [
+                    work.tile([P, HEADS_PER_BANK, HEAD_DIM], F32, bufs=4, tag="rotated", name="rotated_%d" % n)
+                    for n in banks
+                ]
+                for to, source in ((low, high), (high, low)):
+                    for t, u in zip(turned, finished):
+                        nc.vector.tensor_tensor(out=t[:, :, to], in0=u[:, :, source], in1=sin_heads[:, :, to], op=MULT)
+                for r, u in zip(rotated, finished):
+                    nc.vector.tensor_tensor(out=r[:], in0=u[:], in1=cos_heads, op=MULT)
+                for r, t in zip(rotated, turned):
+                    nc.vector.tensor_tensor(out=r[:], in0=r[:], in1=t[:], op=ADD)
+                finished = rotated
+            for n, tile in enumerate(finished):
                 heads = slice(n * HEADS_PER_BANK, (n + 1) * HEADS_PER_BANK)
                 for b in range(BATCH):
                     nc.sync.dma_start(
-                        out=outs[j][b, heads].rearrange("h t d -> t h d"), in_=finished[b:P:BATCH, :, :]
+                        out=outs[j][b, heads].rearrange("h t d -> t h d"), in_=tile[b:P:BATCH, :, :]
                     )

@@ -37,6 +37,8 @@ GROUPS_PER_BANK = 2
 GROUPS_PER_X_LOAD = 4
 GROUPS_PER_SCALE_LOAD = 4
 GROUPS_PER_WORD_LOAD = 2
+WARM_UP_PASSES = 10
+EARLY_GROUPS = 8
 
 FLOPS = 2 * BATCH * SEQ * D_MODEL * QKV_COLS
 
@@ -82,6 +84,19 @@ def tile_causalselfattention_pa_k_kernel(
             nc.gpsimd.dma_start(out=sin_sb[b:P:BATCH, :], in_=rope_sin[0, 0])
         nc.gpsimd.dma_start(out=bias_rows[0:1, :], in_=qkv_b.rearrange("(o n) -> o n", o=1))
 
+        def load_words(j, first, end, first_col=0, end_col=STREAM_COLS):
+            stream_bytes = slice(first_col * FP4_WORD_BYTES, end_col * FP4_WORD_BYTES)
+            row_bytes = slice(
+                (j * STREAM_COLS + first_col) * FP4_WORD_BYTES, (j * STREAM_COLS + end_col) * FP4_WORD_BYTES
+            )
+            nc.sync.dma_start(
+                out=w_words[:, j, first:end, stream_bytes].bitcast(I32),
+                in_=qkv_w_words[first:end, :, row_bytes].bitcast(I32).rearrange("g p n -> p g n"),
+            )
+
+        for g in range(0, EARLY_GROUPS, GROUPS_PER_WORD_LOAD):
+            load_words(0, g, g + GROUPS_PER_WORD_LOAD)
+
         for s in range(GROUPS // GROUPS_PER_SCALE_LOAD):
             groups = slice(s * GROUPS_PER_SCALE_LOAD, (s + 1) * GROUPS_PER_SCALE_LOAD)
             nc.vector.memset(w_scales[s][:].bitcast(I32), 0)
@@ -93,18 +108,16 @@ def tile_causalselfattention_pa_k_kernel(
                 )
 
         for j in range(STREAMS):
-            stream_bytes = slice(
-                j * STREAM_COLS * FP4_WORD_BYTES, (j + 1) * STREAM_COLS * FP4_WORD_BYTES
-            )
-            starts = list(range(0, GROUPS, GROUPS_PER_WORD_LOAD)) + [GROUPS]
-            if j == STREAMS - 1:
-                starts = starts[:-1] + [GROUPS - 1, GROUPS]
-            for first, end in zip(starts[:-1], starts[1:]):
-                groups = slice(first, end)
-                nc.sync.dma_start(
-                    out=w_words[:, j, groups, :].bitcast(I32),
-                    in_=qkv_w_words[groups, :, stream_bytes].bitcast(I32).rearrange("g p n -> p g n"),
-                )
+            first = EARLY_GROUPS + GROUPS_PER_WORD_LOAD if j == 0 else 0
+            end = GROUPS - GROUPS_PER_WORD_LOAD if j == STREAMS - 1 else GROUPS
+            if j == 0:
+                for g in range(EARLY_GROUPS, first):
+                    load_words(j, g, g + 1)
+            for g in range(first, end, GROUPS_PER_WORD_LOAD):
+                load_words(j, g, g + GROUPS_PER_WORD_LOAD)
+        load_words(STREAMS - 1, GROUPS - 2, GROUPS - 1)
+        for n in range(BANKS_PER_STREAM):
+            load_words(STREAMS - 1, GROUPS - 1, GROUPS, n * BANK_COLS, (n + 1) * BANK_COLS)
 
         x_words = x_sb[:].bitcast(F32)
         for c in range(GROUPS // GROUPS_PER_X_LOAD):
@@ -142,12 +155,25 @@ def tile_causalselfattention_pa_k_kernel(
         low = slice(0, HALF_DIM)
         high = slice(HALF_DIM, HEAD_DIM)
 
+        def warm_up():
+            unused = psum.tile([P, BANK_COLS], F32, tag="bank")
+            for i in range(WARM_UP_PASSES):
+                nc.tensor.matmul(
+                    out=unused[:],
+                    lhsT=ones[:],
+                    rhs=bias_rows[:, 0:BANK_COLS],
+                    start=(i == 0),
+                    stop=(i == WARM_UP_PASSES - 1),
+                )
+
         for j in range(STREAMS):
             acc = [
                 psum.tile([P, BANK_COLS], F32, tag="bank", name="acc_%d_%d" % (j, n))
                 for n in range(BANKS_PER_STREAM)
             ]
             for g in range(GROUPS):
+                if j == 0 and g == EARLY_GROUPS:
+                    warm_up()
                 for n in range(BANKS_PER_STREAM):
                     word_bytes = slice(
                         n * BANK_COLS * FP4_WORD_BYTES, (n + 1) * BANK_COLS * FP4_WORD_BYTES

from contextlib import ExitStack

import concourse.mybir as mybir
from concourse.masks import make_identity

F32 = mybir.dt.float32
BF16 = mybir.dt.bfloat16
I32 = mybir.dt.int32
U32 = mybir.dt.uint32
U8 = mybir.dt.uint8
FP8X4 = mybir.dt.float8_e4m3fn_x4
FP4X4 = mybir.dt.float4_e2m1fn_x4
ADD = mybir.AluOpType.add
MULT = mybir.AluOpType.mult

P = 128
PACK = 4
K_PASS = P * PACK

BATCH, SEQ, D_MODEL = 2, 64, 8192
HEADS, HEAD_DIM = 8, 128
HALF_DIM = HEAD_DIM // 2
STREAMS = 3
ROTATED_STREAMS = 2
STREAM_COLS = HEADS * HEAD_DIM
QKV_COLS = STREAMS * STREAM_COLS
GROUPS = D_MODEL // K_PASS

BANK_COLS = 512
BANKS = 8
BANKS_PER_STREAM = STREAM_COLS // BANK_COLS
HEADS_PER_BANK = BANK_COLS // HEAD_DIM
FP4_WORD_BYTES = 2

WORDS_PER_GROUP = K_PASS // 2
GROUPS_PER_BANK = 2
GROUPS_PER_X_LOAD = 4
GROUPS_PER_SCALE_LOAD = 4
GROUPS_PER_WORD_LOAD = 2
WARM_UP_PASSES = 10
EARLY_GROUPS = 8

FLOPS = 2 * BATCH * SEQ * D_MODEL * QKV_COLS


def tile_causalselfattention_pa_k_kernel(
    tc, x, rope_cos, rope_sin, qkv_w_words, qkv_w_scales, qkv_b, out_0, out_1, out_2
):
    nc = tc.nc
    outs = [out_0, out_1, out_2]

    with ExitStack() as ctx:
        ctx.enter_context(tc.manual_schedule())
        keep = ctx.enter_context(tc.tile_pool(name="keep", bufs=1))
        work = ctx.enter_context(tc.tile_pool(name="work", bufs=3))
        psum = ctx.enter_context(tc.psum_pool(name="psum", bufs=BANKS))

        x_sb = keep.tile([P, D_MODEL], BF16)
        x_grouped = keep.tile([P, GROUPS, P, PACK], BF16, align_bytes=64)
        x_codes = keep.tile([P, GROUPS, P], U32, align_bytes=64)
        x_scales = keep.tile([P, GROUPS, P], U8, align_bytes=64)
        w_words = keep.tile([P, STREAMS, GROUPS, STREAM_COLS * FP4_WORD_BYTES], U8, align_bytes=64)
        w_scales = [
            keep.tile([P, GROUPS_PER_SCALE_LOAD, QKV_COLS], U8, align_bytes=64, name="w_scales_%d" % s)
            for s in range(GROUPS // GROUPS_PER_SCALE_LOAD)
        ]
        identity = keep.tile([P, P], F32)
        ones = keep.tile([P, P], BF16)
        bias_rows = keep.tile([P, QKV_COLS], BF16)
        bias_all = keep.tile([P, QKV_COLS], BF16)
        cos_sb = keep.tile([P, HEAD_DIM], BF16)
        sin_sb = keep.tile([P, HEAD_DIM], BF16)

        for c in range(GROUPS // GROUPS_PER_X_LOAD):
            cols = slice(c * GROUPS_PER_X_LOAD * K_PASS, (c + 1) * GROUPS_PER_X_LOAD * K_PASS)
            for b in range(BATCH):
                nc.sync.dma_start(out=x_sb[b:P:BATCH, cols], in_=x[b, :, cols])

        make_identity(nc, identity[:])
        nc.vector.memset(ones[:], 1.0)
        nc.scalar.mul(bias_rows[:], ones[:, 0:1].to_broadcast([P, QKV_COLS]), 0.0)
        for b in range(BATCH):
            nc.gpsimd.dma_start(out=cos_sb[b:P:BATCH, :], in_=rope_cos[0, 0])
            nc.gpsimd.dma_start(out=sin_sb[b:P:BATCH, :], in_=rope_sin[0, 0])
        nc.gpsimd.dma_start(out=bias_rows[0:1, :], in_=qkv_b.rearrange("(o n) -> o n", o=1))

        def load_words(j, first, end, first_col=0, end_col=STREAM_COLS):
            stream_bytes = slice(first_col * FP4_WORD_BYTES, end_col * FP4_WORD_BYTES)
            row_bytes = slice(
                (j * STREAM_COLS + first_col) * FP4_WORD_BYTES, (j * STREAM_COLS + end_col) * FP4_WORD_BYTES
            )
            nc.sync.dma_start(
                out=w_words[:, j, first:end, stream_bytes].bitcast(I32),
                in_=qkv_w_words[first:end, :, row_bytes].bitcast(I32).rearrange("g p n -> p g n"),
            )

        for g in range(0, EARLY_GROUPS, GROUPS_PER_WORD_LOAD):
            load_words(0, g, g + GROUPS_PER_WORD_LOAD)

        for s in range(GROUPS // GROUPS_PER_SCALE_LOAD):
            groups = slice(s * GROUPS_PER_SCALE_LOAD, (s + 1) * GROUPS_PER_SCALE_LOAD)
            nc.vector.memset(w_scales[s][:].bitcast(I32), 0)
            for i in range(8):
                first_partition = 32 * (i // 4) + i % 4
                nc.sync.dma_start(
                    out=w_scales[s][first_partition:P:64, :, :].bitcast(I32),
                    in_=qkv_w_scales[groups, i:16:8, :].bitcast(I32).rearrange("g i n -> i g n"),
                )

        for j in range(STREAMS):
            first = EARLY_GROUPS + GROUPS_PER_WORD_LOAD if j == 0 else 0
            end = GROUPS - GROUPS_PER_WORD_LOAD if j == STREAMS - 1 else GROUPS
            if j == 0:
                for g in range(EARLY_GROUPS, first):
                    load_words(j, g, g + 1)
            for g in range(first, end, GROUPS_PER_WORD_LOAD):
                load_words(j, g, g + GROUPS_PER_WORD_LOAD)
        load_words(STREAMS - 1, GROUPS - 2, GROUPS - 1)
        for n in range(BANKS_PER_STREAM):
            load_words(STREAMS - 1, GROUPS - 1, GROUPS, n * BANK_COLS, (n + 1) * BANK_COLS)

        x_words = x_sb[:].bitcast(F32)
        for c in range(GROUPS // GROUPS_PER_X_LOAD):
            for bank in range(GROUPS_PER_X_LOAD // GROUPS_PER_BANK):
                first_group = c * GROUPS_PER_X_LOAD + bank * GROUPS_PER_BANK
                x_t = psum.tile([P, GROUPS_PER_BANK, 2, P], F32, tag="bank")
                for i in range(GROUPS_PER_BANK):
                    first_word = (first_group + i) * WORDS_PER_GROUP
                    for u in range(2):
                        nc.tensor.transpose(
                            x_t[:, i, u, :],
                            x_words[:, first_word + u : first_word + WORDS_PER_GROUP : 2],
                            identity[:],
                        )
                nc.scalar.copy(
                    out=x_grouped[:, first_group : first_group + GROUPS_PER_BANK, :, :].bitcast(F32),
                    in_=x_t[:].rearrange("p g u r -> p g r u"),
                )
            groups = slice(c * GROUPS_PER_X_LOAD, (c + 1) * GROUPS_PER_X_LOAD)
            nc.vector.quantize_mx(
                out=x_codes[:, groups, :].rearrange("p g r -> p (g r)").bitcast(FP8X4),
                scales=x_scales[:, groups, :].rearrange("p g r -> p (g r)"),
                in_=x_grouped[:, groups, :, :].rearrange("p g r t -> p (g r t)"),
            )

        for n in range(QKV_COLS // BANK_COLS):
            cols = slice(n * BANK_COLS, (n + 1) * BANK_COLS)
            bias_bank = psum.tile([P, BANK_COLS], F32, tag="bank")
            nc.tensor.matmul(out=bias_bank[:], lhsT=ones[:], rhs=bias_rows[:, cols], start=True, stop=True)
            nc.scalar.copy(out=bias_all[:, cols], in_=bias_bank[:])

        nc.vector.tensor_scalar_mul(out=sin_sb[:, 0:HALF_DIM], in0=sin_sb[:, 0:HALF_DIM], scalar1=-1.0)
        cos_heads = cos_sb[:].unsqueeze(1).to_broadcast([P, HEADS_PER_BANK, HEAD_DIM])
        sin_heads = sin_sb[:].unsqueeze(1).to_broadcast([P, HEADS_PER_BANK, HEAD_DIM])
        low = slice(0, HALF_DIM)
        high = slice(HALF_DIM, HEAD_DIM)

        def warm_up():
            unused = psum.tile([P, BANK_COLS], F32, tag="bank")
            for i in range(WARM_UP_PASSES):
                nc.tensor.matmul(
                    out=unused[:],
                    lhsT=ones[:],
                    rhs=bias_rows[:, 0:BANK_COLS],
                    start=(i == 0),
                    stop=(i == WARM_UP_PASSES - 1),
                )

        for j in range(STREAMS):
            acc = [
                psum.tile([P, BANK_COLS], F32, tag="bank", name="acc_%d_%d" % (j, n))
                for n in range(BANKS_PER_STREAM)
            ]
            for g in range(GROUPS):
                if j == 0 and g == EARLY_GROUPS:
                    warm_up()
                for n in range(BANKS_PER_STREAM):
                    word_bytes = slice(
                        n * BANK_COLS * FP4_WORD_BYTES, (n + 1) * BANK_COLS * FP4_WORD_BYTES
                    )
                    qkv_col = j * STREAM_COLS + n * BANK_COLS
                    nc.tensor.matmul_mx(
                        out=acc[n][:],
                        lhsT=x_codes[:, g, :].bitcast(FP8X4),
                        lhsT_scale=x_scales[:, g, :],
                        rhs=w_words[:, j, g, word_bytes].bitcast(FP4X4),
                        rhs_scale=w_scales[g // GROUPS_PER_SCALE_LOAD][:, g % GROUPS_PER_SCALE_LOAD, qkv_col : qkv_col + BANK_COLS],
                        start=(g == 0),
                        stop=(g == GROUPS - 1),
                    )

            banks = range(BANKS_PER_STREAM)
            finished = []
            for n in banks:
                qkv_col = j * STREAM_COLS + n * BANK_COLS
                biased = work.tile([P, HEADS_PER_BANK, HEAD_DIM], F32)
                nc.vector.tensor_tensor(
                    out=biased[:].rearrange("p h d -> p (h d)"),
                    in0=acc[n][:],
                    in1=bias_all[:, qkv_col : qkv_col + BANK_COLS],
                    op=ADD,
                )
                finished.append(biased)
            if j < ROTATED_STREAMS:
                turned = [work.tile([P, HEADS_PER_BANK, HEAD_DIM], F32, tag="turned", name="turned_%d" % n) for n in banks]
                rotated = [
                    work.tile([P, HEADS_PER_BANK, HEAD_DIM], F32, bufs=4, tag="rotated", name="rotated_%d" % n)
                    for n in banks
                ]
                for to, source in ((low, high), (high, low)):
                    for t, u in zip(turned, finished):
                        nc.vector.tensor_tensor(out=t[:, :, to], in0=u[:, :, source], in1=sin_heads[:, :, to], op=MULT)
                for r, u in zip(rotated, finished):
                    nc.vector.tensor_tensor(out=r[:], in0=u[:], in1=cos_heads, op=MULT)
                for r, t in zip(rotated, turned):
                    nc.vector.tensor_tensor(out=r[:], in0=r[:], in1=t[:], op=ADD)
                finished = rotated
            for n, tile in enumerate(finished):
                heads = slice(n * HEADS_PER_BANK, (n + 1) * HEADS_PER_BANK)
                for b in range(BATCH):
                    nc.sync.dma_start(
                        out=outs[j][b, heads].rearrange("h t d -> t h d"), in_=tile[b:P:BATCH, :, :]
                    )
